import numpy as np
import ml_dtypes


def mxq(x, axis, fmt="e4m3"):
    dtype, down = {"e4m3": (ml_dtypes.float8_e4m3fn, 7), "e5m2": (ml_dtypes.float8_e5m2, 14)}[fmt]
    v = np.moveaxis(np.asarray(x, np.float32).astype(ml_dtypes.bfloat16).astype(np.float64), axis, -1)
    blocks = v.reshape(v.shape[:-1] + (-1, 32))
    amax = np.abs(blocks).max(-1, keepdims=True)
    byte = np.maximum(np.where(amax > 0, np.frexp(amax)[1] - 1 + 127, 0) - down, 1)
    scale = np.exp2(byte - 127.0)
    codes = (blocks / scale).astype(np.float32).astype(dtype).astype(np.float64)
    return np.moveaxis((codes * scale).reshape(v.shape), -1, axis)


WIDE = False


def mx_kscale(k):
    if not WIDE:
        return np.ones(k)
    levels = np.array([10, -10, 5, -5, 0])
    a = np.random.permutation(np.resize(levels, k // 512 * 4)).reshape(k // 512, 4)
    idx = np.arange(k)
    return np.exp2(a[idx // 512, idx % 128 // 32])


BF16 = ml_dtypes.bfloat16


def bf(x):
    return np.asarray(x, np.float32).astype(BF16)


def f64(x):
    return np.asarray(x).astype(np.float64)


E2M1 = np.array([0.0, 0.5, 1.0, 1.5, 2.0, 3.0, 4.0, 6.0, -0.0, -0.5, -1.0, -1.5, -2.0, -3.0, -4.0, -6.0])


def pack_weight(w, fmt):
    k, n = w.shape
    w = f64(bf(w)).reshape(k // 32, 32, n)
    amax = np.abs(w).max(1)
    if fmt == "e4m3":
        byte = np.frexp(amax)[1] - 1 + 127 - 7
    else:
        mant, ex = np.frexp(amax / 6.0)
        byte = np.where(mant > 0.5, ex, ex - 1) + 127
    byte = np.clip(np.where(amax > 0, byte, 1), 1, 254)
    scaled = (w * np.exp2(127.0 - byte)[:, None, :]).reshape(k, n).astype(np.float32)
    by_word = np.ascontiguousarray(scaled.reshape(k // 512, 128, 4, n).transpose(0, 1, 3, 2))
    if fmt == "e4m3":
        words = by_word.astype(ml_dtypes.float8_e4m3fn).view(np.uint8)
    else:
        c = by_word.astype(ml_dtypes.float4_e2m1fn).view(np.uint8) & 0xF
        words = c[..., 0::2] | (c[..., 1::2] << 4)
    return np.ascontiguousarray(words), np.ascontiguousarray(byte.astype(np.uint8).reshape(k // 512, 16, n))


def unpack_weight(words, scales, fmt):
    g, p, n, _ = words.shape
    if fmt == "e4m3":
        vals = np.ascontiguousarray(words).view(ml_dtypes.float8_e4m3fn).astype(np.float64)
    else:
        nib = np.empty((g, p, n, 4), np.uint8)
        nib[..., 0::2] = words & 0xF
        nib[..., 1::2] = words >> 4
        vals = E2M1[nib]
    vals = vals * np.repeat(np.exp2(scales.astype(np.float64) - 127.0), 8, axis=1)[..., None]
    return vals.transpose(0, 1, 3, 2).reshape(g * 512, n)

def pack4(w):
    words, scales = pack_weight(w, "e2m1")
    return words.reshape(words.shape[0], 128, -1), scales


def unpack4(words, scales):
    return unpack_weight(words.reshape(words.shape[0], 128, -1, 2), scales, "e2m1")


B, T, KA, KT, DIM, NH, HD, E = 2, 512, 256, 256, 1024, 8, 128, 8
ROPE_BASE = 10000.0


def rope_cos_sin(L, hd):
    inv_freq = 1.0 / (ROPE_BASE ** (f64(np.arange(0, hd, 2)) / hd))
    freqs = f64(np.arange(L))[:, None] * inv_freq[None, :]
    emb = np.concatenate([freqs, freqs], axis=-1)
    return np.cos(emb), np.sin(emb)


def rotate_half(x):
    x1 = x[..., 0::2]
    x2 = x[..., 1::2]
    return np.stack((-x2, x1), axis=-1).reshape(x.shape)


def rope(t, cos, sin):
    return t * cos[None, None] + rotate_half(t) * sin[None, None]


def heads(t):
    return t.reshape(B, -1, NH, HD).transpose(0, 2, 1, 3)


def setup_inputs():
    s = mx_kscale(DIM)
    c = 1.2 / np.sqrt(DIM)
    x = bf(np.random.standard_normal((B, T, DIM)) * s)
    qa_words, qa_scales = pack4((np.random.standard_normal((NH * HD, DIM)) * c / s[None, :]).T)
    b_qa = bf(np.random.standard_normal(NH * HD) * 0.3)
    qt_words, qt_scales = pack4((np.random.standard_normal((NH * HD, DIM)) * c / s[None, :]).T)
    b_qt = bf(np.random.standard_normal(NH * HD) * 0.3)
    return {"x": x,
            "W_qa_words": qa_words,
            "W_qa_scales": qa_scales,
            "b_qa": b_qa,
            "W_qt_words": qt_words,
            "W_qt_scales": qt_scales,
            "b_qt": b_qt}


def reference(x, W_qa_words, W_qa_scales, b_qa, W_qt_words, W_qt_scales, b_qt):
    xq = mxq(f64(x), 2, "e4m3")
    q_a = heads((xq @ unpack4(W_qa_words, W_qa_scales)) + f64(b_qa))
    q_t = heads((xq @ unpack4(W_qt_words, W_qt_scales)) + f64(b_qt))
    cos_m, sin_m = rope_cos_sin(T, HD)
    return rope(q_a, cos_m, sin_m), rope(q_t, cos_m, sin_m)

@@ -1,0 +1,260 @@
+from contextlib import ExitStack
+import math
+
+import concourse.mybir as mybir
+from concourse.masks import make_identity
+
+F32 = mybir.dt.float32
+BF16 = mybir.dt.bfloat16
+I32 = mybir.dt.int32
+U32 = mybir.dt.uint32
+U8 = mybir.dt.uint8
+FP8X4 = mybir.dt.float8_e4m3fn_x4
+FP4X4 = mybir.dt.float4_e2m1fn_x4
+ALU = mybir.AluOpType
+ACT = mybir.ActivationFunctionType
+
+BATCH, TOKENS, DIM, HEADS, HEAD_DIM = 2, 512, 1024, 8, 128
+WEIGHTS = 2
+ROPE_BASE = 10000.0
+
+P = 128
+K_PASS = 4 * P
+PASSES = DIM // K_PASS
+TOK_PER_PART = TOKENS // P
+FREQS = HEAD_DIM // 2
+PAIR = 2
+
+FLOPS = 2 * BATCH * TOKENS * DIM * WEIGHTS * HEADS * HEAD_DIM
+
+ROUND_TO_INT = 1.5 * 2.0**23
+TWO_PI_HIGH = 6.28125
+TWO_PI_LOW = 2.0 * math.pi - TWO_PI_HIGH
+
+
+def tile_l1regressionmoeactionhead_pa_kernel(
+    tc, x, W_qa_words, W_qa_scales, b_qa, W_qt_words, W_qt_scales, b_qt, out_0, out_1
+):
+    nc = tc.nc
+    given = ((W_qa_words, W_qa_scales, b_qa), (W_qt_words, W_qt_scales, b_qt))
+    outs = (out_0, out_1)
+
+    with ExitStack() as ctx:
+        ctx.enter_context(tc.manual_schedule())
+        keep = ctx.enter_context(tc.tile_pool(name="keep", bufs=1))
+        stage = ctx.enter_context(tc.tile_pool(name="stage", bufs=4))
+        rope = ctx.enter_context(tc.tile_pool(name="rope", bufs=3))
+        psum_scalar = ctx.enter_context(tc.psum_pool(name="psum_scalar", bufs=4))
+        psum_vector = ctx.enter_context(tc.psum_pool(name="psum_vector", bufs=4))
+
+        x_sb = keep.tile([P, BATCH, TOK_PER_PART, DIM], BF16)
+        w_words = keep.tile([P, WEIGHTS, PASSES, 2 * HEADS * HEAD_DIM], U8, align_bytes=64)
+        w_planes = keep.tile([P, WEIGHTS, PASSES, HEADS * HEAD_DIM], U8, align_bytes=64)
+        bias_rows = keep.tile([P, P], BF16)
+        zero = keep.tile([P, 1], F32)
+
+        nc.vector.memset(w_planes[:].bitcast(I32), 0)
+        nc.vector.memset(zero[:], 0.0)
+        nc.gpsimd.memset(bias_rows[:], 0.0)
+
+        def load_x(n):
+            rows = x[n].rearrange("(p j) k -> p j k", j=TOK_PER_PART)
+            for j in range(TOK_PER_PART):
+                nc.sync.dma_start(out=x_sb[:, n, j, :], in_=rows[:, j, :])
+
+        def load_weight(w):
+            words, scales, bias = given[w]
+            by_r = scales.bitcast(I32).rearrange("g (q r) n -> r q g n", r=4)
+            for r in range(4):
+                nc.sync.dma_start(out=w_planes[r:P:32, w, :, :].bitcast(I32), in_=by_r[r])
+            nc.sync.dma_start(
+                out=w_words[:, w, :, :].bitcast(I32),
+                in_=words.bitcast(I32).rearrange("g p c -> p g c"),
+            )
+            nc.scalar.dma_start(
+                out=bias_rows[HEADS * w : HEADS * (w + 1), :],
+                in_=bias.rearrange("(h d) -> h d", d=HEAD_DIM),
+            )
+
+        load_x(0)
+        load_weight(0)
+        load_weight(1)
+        load_x(1)
+
+        nc.scalar.activation(out=zero[:], in_=zero[:], func=ACT.Sin)
+
+        token_i = keep.tile([P, TOK_PER_PART], I32)
+        nc.gpsimd.iota(token_i[:], pattern=[[1, TOK_PER_PART]], base=0, channel_multiplier=TOK_PER_PART)
+        ident = keep.tile([P, P], F32)
+        make_identity(nc, ident[:])
+        bias_f32 = keep.tile([P, P], F32)
+        nc.gpsimd.tensor_copy(out=bias_f32[:], in_=bias_rows[:])
+
+        freq = keep.tile([P, FREQS], F32)
+        nc.vector.memset(freq[:, 0:1], 1.0)
+        s = 1
+        while s < FREQS:
+            nc.vector.tensor_scalar(
+                out=freq[:, s : 2 * s], in0=freq[:, 0:s],
+                scalar1=ROPE_BASE ** (-s / FREQS), scalar2=None, op0=ALU.mult,
+            )
+            s *= 2
+
+        table_shape = [P, TOK_PER_PART, FREQS]
+        token_f = keep.tile([P, TOK_PER_PART], F32)
+        nc.vector.tensor_copy(out=token_f[:], in_=token_i[:])
+        angle = keep.tile(table_shape, F32)
+        nc.vector.tensor_tensor(
+            out=angle[:],
+            in0=freq[:].unsqueeze(1).to_broadcast(table_shape),
+            in1=token_f[:].unsqueeze(2).to_broadcast(table_shape),
+            op=ALU.mult,
+        )
+        turns = keep.tile(table_shape, F32)
+        nc.vector.tensor_scalar(
+            out=turns[:], in0=angle[:], scalar1=1.0 / (2.0 * math.pi), scalar2=ROUND_TO_INT,
+            op0=ALU.mult, op1=ALU.add,
+        )
+        nc.vector.tensor_scalar(
+            out=turns[:], in0=turns[:], scalar1=ROUND_TO_INT, scalar2=None, op0=ALU.subtract
+        )
+        flat = "p j m -> p (j m)"
+        part = keep.tile(table_shape, F32)
+        nc.vector.scalar_tensor_tensor(
+            out=part[:].rearrange(flat), in0=turns[:].rearrange(flat), scalar=-TWO_PI_HIGH,
+            in1=angle[:].rearrange(flat), op0=ALU.mult, op1=ALU.add,
+        )
+        reduced = keep.tile(table_shape, F32)
+        nc.vector.scalar_tensor_tensor(
+            out=reduced[:].rearrange(flat), in0=turns[:].rearrange(flat), scalar=-TWO_PI_LOW,
+            in1=part[:].rearrange(flat), op0=ALU.mult, op1=ALU.add,
+        )
+        for_cos = keep.tile(table_shape, F32)
+        nc.vector.scalar_tensor_tensor(
+            out=for_cos[:].rearrange(flat), in0=reduced[:].rearrange(flat), scalar=-1.0,
+            in1=reduced[:].rearrange(flat), op0=ALU.mult, op1=ALU.min,
+        )
+        nc.vector.tensor_scalar(
+            out=for_cos[:], in0=for_cos[:], scalar1=math.pi / 2.0, scalar2=None, op0=ALU.add
+        )
+
+        x_codes = keep.tile([P, BATCH, PASSES, TOKENS], U32, align_bytes=64)
+        x_planes = keep.tile([P, BATCH, PASSES, TOKENS], U8, align_bytes=64)
+
+        def turn_and_quantise(n, j):
+            words = x_sb[:, n, j, :].bitcast(F32)
+            turned = psum_scalar.tile([P, PASSES, 2, P], F32, name="x_turned", tag="scalar")
+            for g in range(PASSES):
+                for u in range(2):
+                    nc.tensor.transpose(
+                        turned[:, g, u, :], words[:, 256 * g + u : 256 * (g + 1) : 2], ident[:]
+                    )
+            grouped = stage.tile([P, PASSES, 4 * P], BF16, name="grouped", align_bytes=64)
+            nc.scalar.copy(
+                out=grouped[:].bitcast(F32).rearrange("p g (t u) -> p g t u", u=2),
+                in_=turned[:].rearrange("p g u t -> p g t u"),
+            )
+            cols = slice(P * j, P * (j + 1))
+            for g in range(PASSES):
+                nc.vector.quantize_mx(
+                    out=x_codes[:, n, g, cols].bitcast(FP8X4),
+                    scales=x_planes[:, n, g, cols],
+                    in_=grouped[:, g, :],
+                )
+
+        for j in range(TOK_PER_PART):
+            turn_and_quantise(0, j)
+
+        bias_turned = psum_scalar.tile([P, P], F32, name="bias_turned", tag="scalar")
+        nc.tensor.transpose(bias_turned[:], bias_f32[:], ident[:])
+        bias_col = keep.tile([P, WEIGHTS * HEADS], F32)
+        nc.scalar.copy(out=bias_col[:], in_=bias_turned[:, 0 : WEIGHTS * HEADS])
+
+        cos_tab = keep.tile([P, TOK_PER_PART, 2, FREQS], F32)
+        nc.scalar.activation(
+            out=cos_tab[:],
+            in_=for_cos[:].unsqueeze(2).to_broadcast([P, TOK_PER_PART, 2, FREQS]),
+            func=ACT.Sin,
+        )
+        sin_tab = keep.tile([P, 2, TOK_PER_PART, 2, FREQS // 2], F32)
+        by_parity = reduced[:].rearrange("p j (i e) -> p e j i", e=2)
+        for e in range(2):
+            nc.scalar.activation(
+                out=sin_tab[:, e],
+                in_=by_parity[:, e].unsqueeze(2).to_broadcast([P, TOK_PER_PART, 2, FREQS // 2]),
+                func=ACT.Sin,
+                scale=(-1.0 if e == 0 else 1.0),
+            )
+
+        def project(n, w, first_head):
+            biased = []
+            for h in range(first_head, first_head + PAIR):
+                acc = psum_scalar.tile([P, TOKENS], F32, name="acc", tag="scalar")
+                for g in range(PASSES):
+                    nc.tensor.matmul_mx(
+                        out=acc[:],
+                        lhsT=w_words[:, w, g, 2 * P * h : 2 * P * (h + 1)].bitcast(FP4X4),
+                        lhsT_scale=w_planes[:, w, g, P * h : P * (h + 1)],
+                        rhs=x_codes[:, n, g, :].bitcast(FP8X4),
+                        rhs_scale=x_planes[:, n, g, :],
+                        start=(g == 0),
+                        stop=(g == PASSES - 1),
+                    )
+                q_t = stage.tile([P, TOKENS], F32, name="q_t")
+                column = HEADS * w + h
+                nc.scalar.activation(
+                    out=q_t[:], in_=acc[:], func=ACT.Identity,
+                    bias=bias_col[:, column : column + 1], scale=1.0,
+                )
+                biased.append(q_t)
+            return biased
+
+        def rotate(n, w, first_head, biased):
+            q_tiles = []
+            for q_t in biased:
+                q = psum_vector.tile([P, TOK_PER_PART, HEAD_DIM], F32, name="q")
+                for j in range(TOK_PER_PART):
+                    nc.tensor.transpose(q[:, j, :], q_t[:, P * j : P * (j + 1)], ident[:])
+                q_tiles.append(q)
+            by_cos = rope.tile([P, PAIR, TOK_PER_PART, HEAD_DIM], F32, name="by_cos")
+            by_sin = rope.tile([P, PAIR, 2, TOK_PER_PART, HEAD_DIM // 2], F32, name="by_sin")
+            for a in range(PAIR):
+                q = q_tiles[a]
+                nc.vector.tensor_tensor(
+                    out=by_cos[:, a], in0=q[:], in1=cos_tab[:].rearrange("p j s m -> p j (s m)"),
+                    op=ALU.mult,
+                )
+                q_parity = q[:].rearrange("p j (i e) -> p e j i", e=2)
+                for e in range(2):
+                    nc.vector.tensor_tensor(
+                        out=by_sin[:, a, e], in0=q_parity[:, 1 - e],
+                        in1=sin_tab[:, e].rearrange("p j s i -> p j (s i)"), op=ALU.mult,
+                    )
+            result = rope.tile([P, PAIR, TOK_PER_PART * HEAD_DIM], F32, name="result")
+            nc.gpsimd.tensor_tensor(
+                out=result[:].rearrange("p a (c e) -> p a c e", e=2),
+                in0=by_cos[:].rearrange("p a j (i e) -> p a (j i) e", e=2),
+                in1=by_sin[:].rearrange("p a e j i -> p a (j i) e"),
+                op=ALU.add,
+            )
+            nc.sync.dma_start(
+                out=outs[w][n, first_head : first_head + PAIR].rearrange(
+                    "h (p j) d -> p h (j d)", j=TOK_PER_PART
+                ),
+                in_=result[:],
+            )
+
+        groups = [
+            (n, w, first_head)
+            for n in range(BATCH)
+            for w in range(WEIGHTS)
+            for first_head in range(0, HEADS, PAIR)
+        ]
+        waiting = project(*groups[0])
+        for i in range(1, len(groups)):
+            projected = project(*groups[i])
+            rotate(*groups[i - 1], waiting)
+            if i <= TOK_PER_PART:
+                turn_and_quantise(1, i - 1)
+            waiting = projected
+        rotate(*groups[-1], waiting)

@@ -24,6 +24,8 @@ PASSES = DIM // K_PASS
 TOK_PER_PART = TOKENS // P
 FREQS = HEAD_DIM // 2
 PAIR = 2
+COUPLES = TOK_PER_PART * HEAD_DIM // 2
+GPSIMD_ADDS = 208
 
 FLOPS = 2 * BATCH * TOKENS * DIM * WEIGHTS * HEADS * HEAD_DIM
 
@@ -216,32 +218,38 @@ def tile_l1regressionmoeactionhead_pa_kernel(
                 for j in range(TOK_PER_PART):
                     nc.tensor.transpose(q[:, j, :], q_t[:, P * j : P * (j + 1)], ident[:])
                 q_tiles.append(q)
-            by_cos = rope.tile([P, PAIR, TOK_PER_PART, HEAD_DIM], F32, name="by_cos")
-            by_sin = rope.tile([P, PAIR, 2, TOK_PER_PART, HEAD_DIM // 2], F32, name="by_sin")
+            by_cos = rope.tile([P, PAIR, COUPLES, 2], F32, name="by_cos")
+            by_sin = rope.tile([P, PAIR, 2, COUPLES], F32, name="by_sin")
             for a in range(PAIR):
                 q = q_tiles[a]
                 nc.vector.tensor_tensor(
-                    out=by_cos[:, a], in0=q[:], in1=cos_tab[:].rearrange("p j s m -> p j (s m)"),
+                    out=by_cos[:, a].rearrange("p c e -> p (c e)"),
+                    in0=q[:].rearrange("p j d -> p (j d)"),
+                    in1=cos_tab[:].rearrange("p j s m -> p (j s m)"),
                     op=ALU.mult,
                 )
-                q_parity = q[:].rearrange("p j (i e) -> p e j i", e=2)
+                q_parity = q[:].rearrange("p j (i e) -> p e (j i)", e=2)
                 for e in range(2):
                     nc.vector.tensor_tensor(
                         out=by_sin[:, a, e], in0=q_parity[:, 1 - e],
-                        in1=sin_tab[:, e].rearrange("p j s i -> p j (s i)"), op=ALU.mult,
+                        in1=sin_tab[:, e].rearrange("p j s i -> p (j s i)"), op=ALU.mult,
                     )
-            result = rope.tile([P, PAIR, TOK_PER_PART * HEAD_DIM], F32, name="result")
-            nc.gpsimd.tensor_tensor(
-                out=result[:].rearrange("p a (c e) -> p a c e", e=2),
-                in0=by_cos[:].rearrange("p a j (i e) -> p a (j i) e", e=2),
-                in1=by_sin[:].rearrange("p a e j i -> p a (j i) e"),
-                op=ALU.add,
-            )
+            result = rope.tile([P, PAIR, COUPLES, 2], F32, name="result")
+            for engine, share in (
+                (nc.gpsimd, slice(0, GPSIMD_ADDS)),
+                (nc.vector, slice(GPSIMD_ADDS, COUPLES)),
+            ):
+                engine.tensor_tensor(
+                    out=result[:, :, share, :],
+                    in0=by_cos[:, :, share, :],
+                    in1=by_sin[:, :, :, share].rearrange("p a e c -> p a c e"),
+                    op=ALU.add,
+                )
             nc.sync.dma_start(
                 out=outs[w][n, first_head : first_head + PAIR].rearrange(
                     "h (p j) d -> p h (j d)", j=TOK_PER_PART
                 ),
-                in_=result[:],
+                in_=result[:].rearrange("p a c e -> p a (c e)"),
             )
 
         groups = [

@@ -25,13 +25,11 @@ TOK_PER_PART = TOKENS // P
 FREQS = HEAD_DIM // 2
 PAIR = 2
 COUPLES = TOK_PER_PART * HEAD_DIM // 2
-GPSIMD_ADDS = 208
 
 FLOPS = 2 * BATCH * TOKENS * DIM * WEIGHTS * HEADS * HEAD_DIM
 
 ROUND_TO_INT = 1.5 * 2.0**23
-TWO_PI_HIGH = 6.28125
-TWO_PI_LOW = 2.0 * math.pi - TWO_PI_HIGH
+TWO_PI = 2.0 * math.pi
 
 
 def tile_l1regressionmoeactionhead_pa_kernel(
@@ -105,39 +103,32 @@ def tile_l1regressionmoeactionhead_pa_kernel(
         table_shape = [P, TOK_PER_PART, FREQS]
         token_f = keep.tile([P, TOK_PER_PART], F32)
         nc.vector.tensor_copy(out=token_f[:], in_=token_i[:])
-        angle = keep.tile(table_shape, F32)
-        nc.vector.tensor_tensor(
-            out=angle[:],
-            in0=freq[:].unsqueeze(1).to_broadcast(table_shape),
-            in1=token_f[:].unsqueeze(2).to_broadcast(table_shape),
-            op=ALU.mult,
-        )
         turns = keep.tile(table_shape, F32)
-        nc.vector.tensor_scalar(
-            out=turns[:], in0=angle[:], scalar1=1.0 / (2.0 * math.pi), scalar2=ROUND_TO_INT,
-            op0=ALU.mult, op1=ALU.add,
+        nc.vector.scalar_tensor_tensor(
+            out=turns[:],
+            in0=freq[:].unsqueeze(1).to_broadcast(table_shape),
+            scalar=1.0 / TWO_PI,
+            in1=token_f[:].unsqueeze(2).to_broadcast(table_shape),
+            op0=ALU.mult,
+            op1=ALU.mult,
         )
+        shifted = keep.tile(table_shape, F32)
         nc.vector.tensor_scalar(
-            out=turns[:], in0=turns[:], scalar1=ROUND_TO_INT, scalar2=None, op0=ALU.subtract
+            out=shifted[:], in0=turns[:], scalar1=ROUND_TO_INT, scalar2=None, op0=ALU.add
         )
         flat = "p j m -> p (j m)"
-        part = keep.tile(table_shape, F32)
+        minus_frac = keep.tile(table_shape, F32)
         nc.vector.scalar_tensor_tensor(
-            out=part[:].rearrange(flat), in0=turns[:].rearrange(flat), scalar=-TWO_PI_HIGH,
-            in1=angle[:].rearrange(flat), op0=ALU.mult, op1=ALU.add,
-        )
-        reduced = keep.tile(table_shape, F32)
-        nc.vector.scalar_tensor_tensor(
-            out=reduced[:].rearrange(flat), in0=turns[:].rearrange(flat), scalar=-TWO_PI_LOW,
-            in1=part[:].rearrange(flat), op0=ALU.mult, op1=ALU.add,
+            out=minus_frac[:].rearrange(flat), in0=shifted[:].rearrange(flat), scalar=ROUND_TO_INT,
+            in1=turns[:].rearrange(flat), op0=ALU.subtract, op1=ALU.subtract,
         )
         for_cos = keep.tile(table_shape, F32)
         nc.vector.scalar_tensor_tensor(
-            out=for_cos[:].rearrange(flat), in0=reduced[:].rearrange(flat), scalar=-1.0,
-            in1=reduced[:].rearrange(flat), op0=ALU.mult, op1=ALU.min,
+            out=for_cos[:].rearrange(flat), in0=minus_frac[:].rearrange(flat), scalar=-1.0,
+            in1=minus_frac[:].rearrange(flat), op0=ALU.mult, op1=ALU.min,
         )
         nc.vector.tensor_scalar(
-            out=for_cos[:], in0=for_cos[:], scalar1=math.pi / 2.0, scalar2=None, op0=ALU.add
+            out=for_cos[:], in0=for_cos[:], scalar1=0.25, scalar2=None, op0=ALU.add
         )
 
         x_codes = keep.tile([P, BATCH, PASSES, TOKENS], U32, align_bytes=64)
@@ -172,20 +163,22 @@ def tile_l1regressionmoeactionhead_pa_kernel(
         bias_col = keep.tile([P, WEIGHTS * HEADS], F32)
         nc.scalar.copy(out=bias_col[:], in_=bias_turned[:, 0 : WEIGHTS * HEADS])
 
-        cos_tab = keep.tile([P, TOK_PER_PART, 2, FREQS], F32)
+        tables = keep.tile([P, 2, TOK_PER_PART, 2, FREQS], F32)
+        cos_tab = tables[:, 0]
         nc.scalar.activation(
-            out=cos_tab[:],
+            out=cos_tab,
             in_=for_cos[:].unsqueeze(2).to_broadcast([P, TOK_PER_PART, 2, FREQS]),
             func=ACT.Sin,
+            scale=TWO_PI,
         )
-        sin_tab = keep.tile([P, 2, TOK_PER_PART, 2, FREQS // 2], F32)
-        by_parity = reduced[:].rearrange("p j (i e) -> p e j i", e=2)
+        sin_tab = tables[:, 1].rearrange("p j s (i e) -> p e j s i", e=2)
+        by_parity = minus_frac[:].rearrange("p j (i e) -> p e j i", e=2)
         for e in range(2):
             nc.scalar.activation(
                 out=sin_tab[:, e],
-                in_=by_parity[:, e].unsqueeze(2).to_broadcast([P, TOK_PER_PART, 2, FREQS // 2]),
+                in_=by_parity[:, 1 - e].unsqueeze(2).to_broadcast([P, TOK_PER_PART, 2, FREQS // 2]),
                 func=ACT.Sin,
-                scale=(-1.0 if e == 0 else 1.0),
+                scale=(-TWO_PI if e == 0 else TWO_PI),
             )
 
         def project(n, w, first_head):
@@ -211,46 +204,44 @@ def tile_l1regressionmoeactionhead_pa_kernel(
                 biased.append(q_t)
             return biased
 
-        def rotate(n, w, first_head, biased):
+        def rotate(n, w, first_head, biased, last):
             q_tiles = []
             for q_t in biased:
                 q = psum_vector.tile([P, TOK_PER_PART, HEAD_DIM], F32, name="q")
                 for j in range(TOK_PER_PART):
                     nc.tensor.transpose(q[:, j, :], q_t[:, P * j : P * (j + 1)], ident[:])
                 q_tiles.append(q)
-            by_cos = rope.tile([P, PAIR, COUPLES, 2], F32, name="by_cos")
-            by_sin = rope.tile([P, PAIR, 2, COUPLES], F32, name="by_sin")
+            products = rope.tile([P, PAIR, 2, COUPLES, 2], F32, name="products")
             for a in range(PAIR):
-                q = q_tiles[a]
                 nc.vector.tensor_tensor(
-                    out=by_cos[:, a].rearrange("p c e -> p (c e)"),
-                    in0=q[:].rearrange("p j d -> p (j d)"),
-                    in1=cos_tab[:].rearrange("p j s m -> p (j s m)"),
+                    out=products[:, a].rearrange("p k c e -> p k (c e)"),
+                    in0=q_tiles[a][:]
+                    .rearrange("p j d -> p (j d)")
+                    .unsqueeze(1)
+                    .to_broadcast([P, 2, TOK_PER_PART * HEAD_DIM]),
+                    in1=tables[:].rearrange("p k j s m -> p k (j s m)"),
                     op=ALU.mult,
                 )
-                q_parity = q[:].rearrange("p j (i e) -> p e (j i)", e=2)
-                for e in range(2):
-                    nc.vector.tensor_tensor(
-                        out=by_sin[:, a, e], in0=q_parity[:, 1 - e],
-                        in1=sin_tab[:, e].rearrange("p j s i -> p (j s i)"), op=ALU.mult,
-                    )
             result = rope.tile([P, PAIR, COUPLES, 2], F32, name="result")
-            for engine, share in (
-                (nc.gpsimd, slice(0, GPSIMD_ADDS)),
-                (nc.vector, slice(GPSIMD_ADDS, COUPLES)),
-            ):
+
+            def add(engine, heads):
                 engine.tensor_tensor(
-                    out=result[:, :, share, :],
-                    in0=by_cos[:, :, share, :],
-                    in1=by_sin[:, :, :, share].rearrange("p a e c -> p a c e"),
+                    out=result[:, heads],
+                    in0=products[:, heads, 0],
+                    in1=products[:, heads, 1, :, ::-1],
                     op=ALU.add,
                 )
-            nc.sync.dma_start(
-                out=outs[w][n, first_head : first_head + PAIR].rearrange(
-                    "h (p j) d -> p h (j d)", j=TOK_PER_PART
-                ),
-                in_=result[:].rearrange("p a c e -> p a (c e)"),
-            )
+
+            if last:
+                add(nc.gpsimd, slice(0, 1))
+                add(nc.vector, slice(1, PAIR))
+            else:
+                add(nc.gpsimd, slice(0, PAIR))
+            for a in range(PAIR):
+                nc.sync.dma_start(
+                    out=outs[w][n, first_head + a].rearrange("(p j) d -> p (j d)", j=TOK_PER_PART),
+                    in_=result[:, a].rearrange("p c e -> p (c e)"),
+                )
 
         groups = [
             (n, w, first_head)
@@ -258,11 +249,12 @@ def tile_l1regressionmoeactionhead_pa_kernel(
             for w in range(WEIGHTS)
             for first_head in range(0, HEADS, PAIR)
         ]
-        waiting = project(*groups[0])
-        for i in range(1, len(groups)):
+        rotate(*groups[0], project(*groups[0]), False)
+        waiting = project(*groups[1])
+        for i in range(2, len(groups)):
             projected = project(*groups[i])
-            rotate(*groups[i - 1], waiting)
-            if i <= TOK_PER_PART:
-                turn_and_quantise(1, i - 1)
+            rotate(*groups[i - 1], waiting, False)
+            if i - 2 < TOK_PER_PART:
+                turn_and_quantise(1, i - 2)
             waiting = projected
-        rotate(*groups[-1], waiting)
+        rotate(*groups[-1], waiting, True)

@@ -25,6 +25,7 @@ TOK_PER_PART = TOKENS // P
 FREQS = HEAD_DIM // 2
 PAIR = 2
 COUPLES = TOK_PER_PART * HEAD_DIM // 2
+VECTOR_FINISHES = 2
 
 FLOPS = 2 * BATCH * TOKENS * DIM * WEIGHTS * HEADS * HEAD_DIM
 
@@ -91,12 +92,13 @@ def tile_l1regressionmoeactionhead_pa_kernel(
         nc.gpsimd.tensor_copy(out=bias_f32[:], in_=bias_rows[:])
 
         freq = keep.tile([P, FREQS], F32)
-        nc.vector.memset(freq[:, 0:1], 1.0)
+        nc.vector.memset(freq[:, 0:1], -1.0)
         s = 1
         while s < FREQS:
+            factor = ROPE_BASE ** (-s / FREQS)
             nc.vector.tensor_scalar(
                 out=freq[:, s : 2 * s], in0=freq[:, 0:s],
-                scalar1=ROPE_BASE ** (-s / FREQS), scalar2=None, op0=ALU.mult,
+                scalar1=(-factor if s == 1 else factor), scalar2=None, op0=ALU.mult,
             )
             s *= 2
 
@@ -171,14 +173,14 @@ def tile_l1regressionmoeactionhead_pa_kernel(
             func=ACT.Sin,
             scale=TWO_PI,
         )
-        sin_tab = tables[:, 1].rearrange("p j s (i e) -> p e j s i", e=2)
-        by_parity = minus_frac[:].rearrange("p j (i e) -> p e j i", e=2)
-        for e in range(2):
+        sin_tab = tables[:, 1]
+        neighbour = minus_frac[:].rearrange("p j (i e) -> p j i e", e=2)[:, :, :, ::-1]
+        for half in range(2):
             nc.scalar.activation(
-                out=sin_tab[:, e],
-                in_=by_parity[:, 1 - e].unsqueeze(2).to_broadcast([P, TOK_PER_PART, 2, FREQS // 2]),
+                out=sin_tab[:, :, half, :].rearrange("p j (i e) -> p j i e", e=2),
+                in_=neighbour,
                 func=ACT.Sin,
-                scale=(-TWO_PI if e == 0 else TWO_PI),
+                scale=-TWO_PI,
             )
 
         def project(n, w, first_head):
@@ -204,7 +206,7 @@ def tile_l1regressionmoeactionhead_pa_kernel(
                 biased.append(q_t)
             return biased
 
-        def rotate(n, w, first_head, biased, last):
+        def multiply(biased):
             q_tiles = []
             for q_t in biased:
                 q = psum_vector.tile([P, TOK_PER_PART, HEAD_DIM], F32, name="q")
@@ -222,26 +224,25 @@ def tile_l1regressionmoeactionhead_pa_kernel(
                     in1=tables[:].rearrange("p k j s m -> p k (j s m)"),
                     op=ALU.mult,
                 )
-            result = rope.tile([P, PAIR, COUPLES, 2], F32, name="result")
+            return products
 
-            def add(engine, heads):
+        def finish(engine, heads_at_once, n, w, first_head, products):
+            result = rope.tile([P, PAIR, COUPLES, 2], F32, name="result")
+            for first in range(0, PAIR, heads_at_once):
+                heads = slice(first, first + heads_at_once)
                 engine.tensor_tensor(
                     out=result[:, heads],
                     in0=products[:, heads, 0],
                     in1=products[:, heads, 1, :, ::-1],
                     op=ALU.add,
                 )
-
-            if last:
-                add(nc.gpsimd, slice(0, 1))
-                add(nc.vector, slice(1, PAIR))
-            else:
-                add(nc.gpsimd, slice(0, PAIR))
-            for a in range(PAIR):
-                nc.sync.dma_start(
-                    out=outs[w][n, first_head + a].rearrange("(p j) d -> p (j d)", j=TOK_PER_PART),
-                    in_=result[:, a].rearrange("p c e -> p (c e)"),
-                )
+                for a in range(first, first + heads_at_once):
+                    nc.sync.dma_start(
+                        out=outs[w][n, first_head + a].rearrange(
+                            "(p j) d -> p (j d)", j=TOK_PER_PART
+                        ),
+                        in_=result[:, a].rearrange("p c e -> p (c e)"),
+                    )
 
         groups = [
             (n, w, first_head)
@@ -249,12 +250,23 @@ def tile_l1regressionmoeactionhead_pa_kernel(
             for w in range(WEIGHTS)
             for first_head in range(0, HEADS, PAIR)
         ]
-        rotate(*groups[0], project(*groups[0]), False)
+        left_to_vector = []
+
+        def rotate(i, biased):
+            products = multiply(biased)
+            if i < len(groups) - VECTOR_FINISHES:
+                finish(nc.gpsimd, PAIR, *groups[i], products)
+            else:
+                left_to_vector.append((i, products))
+
+        rotate(0, project(*groups[0]))
         waiting = project(*groups[1])
         for i in range(2, len(groups)):
             projected = project(*groups[i])
-            rotate(*groups[i - 1], waiting, False)
+            rotate(i - 1, waiting)
             if i - 2 < TOK_PER_PART:
                 turn_and_quantise(1, i - 2)
             waiting = projected
-        rotate(*groups[-1], waiting, True)
+        rotate(len(groups) - 1, waiting)
+        for i, products in left_to_vector:
+            finish(nc.vector, 1, *groups[i], products)

@@ -26,6 +26,8 @@ FREQS = HEAD_DIM // 2
 PAIR = 2
 COUPLES = TOK_PER_PART * HEAD_DIM // 2
 VECTOR_FINISHES = 2
+IDLE_BEFORE_X = 5
+IDLE_BEFORE_MX = 3
 
 FLOPS = 2 * BATCH * TOKENS * DIM * WEIGHTS * HEADS * HEAD_DIM
 
@@ -53,6 +55,18 @@ def tile_l1regressionmoeactionhead_pa_kernel(
         w_planes = keep.tile([P, WEIGHTS, PASSES, HEADS * HEAD_DIM], U8, align_bytes=64)
         bias_rows = keep.tile([P, P], BF16)
         zero = keep.tile([P, 1], F32)
+
+        idle_in = keep.tile([P, TOKENS], BF16)
+        nc.vector.memset(idle_in[:], 0.0)
+
+        def keep_tensor_engine_busy(times):
+            for i in range(times):
+                idle_out = psum_vector.tile([P, TOKENS], F32, name="idle_out", tag="q")
+                nc.tensor.matmul(
+                    out=idle_out[:], lhsT=idle_in[:, 0:P], rhs=idle_in[:], start=True, stop=True
+                )
+
+        keep_tensor_engine_busy(IDLE_BEFORE_X)
 
         nc.vector.memset(w_planes[:].bitcast(I32), 0)
         nc.vector.memset(zero[:], 0.0)
@@ -159,9 +173,11 @@ def tile_l1regressionmoeactionhead_pa_kernel(
 
         for j in range(TOK_PER_PART):
             turn_and_quantise(0, j)
+            keep_tensor_engine_busy(1)
 
         bias_turned = psum_scalar.tile([P, P], F32, name="bias_turned", tag="scalar")
         nc.tensor.transpose(bias_turned[:], bias_f32[:], ident[:])
+        keep_tensor_engine_busy(IDLE_BEFORE_MX)
         bias_col = keep.tile([P, WEIGHTS * HEADS], F32)
         nc.scalar.copy(out=bias_col[:], in_=bias_turned[:, 0 : WEIGHTS * HEADS])
 

@@ -25,7 +25,7 @@ TOK_PER_PART = TOKENS // P
 FREQS = HEAD_DIM // 2
 PAIR = 2
 COUPLES = TOK_PER_PART * HEAD_DIM // 2
-VECTOR_FINISHES = 2
+TENSOR_ADDS = 2
 IDLE_BEFORE_X = 5
 IDLE_BEFORE_MX = 3
 
@@ -47,6 +47,7 @@ def tile_l1regressionmoeactionhead_pa_kernel(
         keep = ctx.enter_context(tc.tile_pool(name="keep", bufs=1))
         stage = ctx.enter_context(tc.tile_pool(name="stage", bufs=4))
         rope = ctx.enter_context(tc.tile_pool(name="rope", bufs=3))
+        turned = ctx.enter_context(tc.tile_pool(name="turned", bufs=4))
         psum_scalar = ctx.enter_context(tc.psum_pool(name="psum_scalar", bufs=4))
         psum_vector = ctx.enter_context(tc.psum_pool(name="psum_vector", bufs=4))
 
@@ -145,6 +146,12 @@ def tile_l1regressionmoeactionhead_pa_kernel(
         )
         nc.vector.tensor_scalar(
             out=for_cos[:], in0=for_cos[:], scalar1=0.25, scalar2=None, op0=ALU.add
+        )
+
+        swap = keep.tile([P, P], F32)
+        nc.vector.tensor_copy(
+            out=swap[:].rearrange("p (c e) -> p c e", e=2),
+            in_=ident[:].rearrange("p (c e) -> p c e", e=2)[:, :, ::-1],
         )
 
         x_codes = keep.tile([P, BATCH, PASSES, TOKENS], U32, align_bytes=64)
@@ -260,29 +267,137 @@ def tile_l1regressionmoeactionhead_pa_kernel(
                         in_=result[:, a].rearrange("p c e -> p (c e)"),
                     )
 
+        tables_turned = keep.tile([P, 2, TOKENS], F32)
+
+        def turn_tables():
+            for k in range(2):
+                bank = psum_scalar.tile([P, TOK_PER_PART, P], F32, name="table_bank", tag="scalar")
+                for j in range(TOK_PER_PART):
+                    nc.tensor.transpose(
+                        bank[:, j, :], tables[:, k, j].rearrange("p s m -> p (s m)"), ident[:]
+                    )
+                nc.scalar.copy(
+                    out=tables_turned[:, k, :], in_=bank[:].rearrange("p j t -> p (j t)")
+                )
+
+        def turned_project(n, w, first_head):
+            sums = []
+            for h in range(first_head, first_head + PAIR):
+                acc = psum_vector.tile([P, TOKENS], F32, name="acc_v", tag="q")
+                for g in range(PASSES):
+                    nc.tensor.matmul_mx(
+                        out=acc[:],
+                        lhsT=w_words[:, w, g, 2 * P * h : 2 * P * (h + 1)].bitcast(FP4X4),
+                        lhsT_scale=w_planes[:, w, g, P * h : P * (h + 1)],
+                        rhs=x_codes[:, n, g, :].bitcast(FP8X4),
+                        rhs_scale=x_planes[:, n, g, :],
+                        start=(g == 0),
+                        stop=(g == PASSES - 1),
+                    )
+                sums.append(acc)
+            return sums
+
+        def turned_multiply(n, w, first_head, sums, size=PAIR):
+            made = []
+            for a in range(size):
+                column = HEADS * w + first_head + a
+                both = turned.tile([P, 2, TOKENS], F32, name="both")
+                nc.vector.scalar_tensor_tensor(
+                    out=both[:],
+                    in0=sums[a][:].unsqueeze(1).to_broadcast([P, 2, TOKENS]),
+                    scalar=bias_col[:, column : column + 1],
+                    in1=tables_turned[:],
+                    op0=ALU.add,
+                    op1=ALU.mult,
+                )
+                made.append(both)
+            return made
+
+        def turned_finish(n, w, first_head, made, size=PAIR):
+            for a in range(size):
+                summed = psum_scalar.tile([P, TOK_PER_PART, HEAD_DIM], F32, name="summed", tag="scalar")
+                for j in range(TOK_PER_PART):
+                    cols = slice(P * j, P * (j + 1))
+                    nc.tensor.matmul(
+                        out=summed[:, j, :], lhsT=made[a][:, 0, cols], rhs=ident[:],
+                        is_transpose=True, start=True, stop=False,
+                    )
+                    nc.tensor.matmul(
+                        out=summed[:, j, :], lhsT=made[a][:, 1, cols], rhs=swap[:],
+                        is_transpose=True, start=False, stop=True,
+                    )
+                turned_result = turned.tile([P, TOK_PER_PART * HEAD_DIM], F32, name="turned_result")
+                nc.scalar.copy(out=turned_result[:], in_=summed[:].rearrange("p j d -> p (j d)"))
+                nc.sync.dma_start(
+                    out=outs[w][n, first_head + a].rearrange("(p j) d -> p (j d)", j=TOK_PER_PART),
+                    in_=turned_result[:],
+                )
+
+        def turned_in_pieces(n, w, h, acc):
+            column = HEADS * w + h
+            rows = outs[w][n, h].rearrange("(p j) d -> p j d", j=TOK_PER_PART)
+            for j in range(TOK_PER_PART):
+                cols = slice(P * j, P * (j + 1))
+                piece = turned.tile([P, 2, P], F32, name="piece")
+                nc.vector.scalar_tensor_tensor(
+                    out=piece[:],
+                    in0=acc[:, cols].unsqueeze(1).to_broadcast([P, 2, P]),
+                    scalar=bias_col[:, column : column + 1],
+                    in1=tables_turned[:, :, cols],
+                    op0=ALU.add,
+                    op1=ALU.mult,
+                )
+                summed = psum_scalar.tile([P, HEAD_DIM], F32, name="summed_piece", tag="scalar")
+                nc.tensor.matmul(
+                    out=summed[:], lhsT=piece[:, 0, :], rhs=ident[:],
+                    is_transpose=True, start=True, stop=False,
+                )
+                nc.tensor.matmul(
+                    out=summed[:], lhsT=piece[:, 1, :], rhs=swap[:],
+                    is_transpose=True, start=False, stop=True,
+                )
+                piece_result = turned.tile([P, HEAD_DIM], F32, name="piece_result")
+                nc.scalar.copy(out=piece_result[:], in_=summed[:])
+                nc.sync.dma_start(out=rows[:, j, :], in_=piece_result[:])
+
         groups = [
             (n, w, first_head)
             for n in range(BATCH)
             for w in range(WEIGHTS)
             for first_head in range(0, HEADS, PAIR)
         ]
-        left_to_vector = []
+        last = len(groups) - 1
+        first_turned = len(groups) - TENSOR_ADDS
 
-        def rotate(i, biased):
-            products = multiply(biased)
-            if i < len(groups) - VECTOR_FINISHES:
-                finish(nc.gpsimd, PAIR, *groups[i], products)
-            else:
-                left_to_vector.append((i, products))
+        def step_one(i):
+            if i < first_turned:
+                return project(*groups[i])
+            return turned_project(*groups[i])
 
-        rotate(0, project(*groups[0]))
-        waiting = project(*groups[1])
+        def step_two(i, projected):
+            if i < first_turned:
+                finish(nc.gpsimd, PAIR, *groups[i], multiply(projected))
+                return None
+            return turned_multiply(*groups[i], projected)
+
+        def step_three(i, made):
+            if made is not None:
+                turned_finish(*groups[i], made)
+
+        step_two(0, step_one(0))
+        waiting = step_one(1)
+        made_before = None
         for i in range(2, len(groups)):
-            projected = project(*groups[i])
-            rotate(i - 1, waiting)
+            projected = step_one(i)
+            made = step_two(i - 1, waiting)
+            step_three(i - 2, made_before)
             if i - 2 < TOK_PER_PART:
                 turn_and_quantise(1, i - 2)
+            if i == TOK_PER_PART + 2:
+                turn_tables()
             waiting = projected
-        rotate(len(groups) - 1, waiting)
-        for i, products in left_to_vector:
-            finish(nc.vector, 1, *groups[i], products)
+            made_before = made
+        made = turned_multiply(*groups[last], waiting, 1)
+        step_three(last - 1, made_before)
+        turned_finish(*groups[last], made, 1)
+        turned_in_pieces(groups[last][0], groups[last][1], groups[last][2] + 1, waiting[1])

@@ -25,7 +25,7 @@ TOK_PER_PART = TOKENS // P
 FREQS = HEAD_DIM // 2
 PAIR = 2
 COUPLES = TOK_PER_PART * HEAD_DIM // 2
-TENSOR_ADDS = 2
+TENSOR_ADDS = 3
 IDLE_BEFORE_X = 5
 IDLE_BEFORE_MX = 3
 
@@ -47,7 +47,7 @@ def tile_l1regressionmoeactionhead_pa_kernel(
         keep = ctx.enter_context(tc.tile_pool(name="keep", bufs=1))
         stage = ctx.enter_context(tc.tile_pool(name="stage", bufs=4))
         rope = ctx.enter_context(tc.tile_pool(name="rope", bufs=3))
-        turned = ctx.enter_context(tc.tile_pool(name="turned", bufs=4))
+        turned = ctx.enter_context(tc.tile_pool(name="turned", bufs=6))
         psum_scalar = ctx.enter_context(tc.psum_pool(name="psum_scalar", bufs=4))
         psum_vector = ctx.enter_context(tc.psum_pool(name="psum_vector", bufs=4))
 

from contextlib import ExitStack
import math

import concourse.mybir as mybir
from concourse.masks import make_identity

F32 = mybir.dt.float32
BF16 = mybir.dt.bfloat16
I32 = mybir.dt.int32
U32 = mybir.dt.uint32
U8 = mybir.dt.uint8
FP8X4 = mybir.dt.float8_e4m3fn_x4
FP4X4 = mybir.dt.float4_e2m1fn_x4
ALU = mybir.AluOpType
ACT = mybir.ActivationFunctionType

BATCH, TOKENS, DIM, HEADS, HEAD_DIM = 2, 512, 1024, 8, 128
WEIGHTS = 2
ROPE_BASE = 10000.0

P = 128
K_PASS = 4 * P
PASSES = DIM // K_PASS
TOK_PER_PART = TOKENS // P
FREQS = HEAD_DIM // 2
PAIR = 2
COUPLES = TOK_PER_PART * HEAD_DIM // 2
TENSOR_ADDS = 3
IDLE_BEFORE_X = 5
IDLE_BEFORE_MX = 3

FLOPS = 2 * BATCH * TOKENS * DIM * WEIGHTS * HEADS * HEAD_DIM

ROUND_TO_INT = 1.5 * 2.0**23
TWO_PI = 2.0 * math.pi


def tile_l1regressionmoeactionhead_pa_kernel(
    tc, x, W_qa_words, W_qa_scales, b_qa, W_qt_words, W_qt_scales, b_qt, out_0, out_1
):
    nc = tc.nc
    given = ((W_qa_words, W_qa_scales, b_qa), (W_qt_words, W_qt_scales, b_qt))
    outs = (out_0, out_1)

    with ExitStack() as ctx:
        ctx.enter_context(tc.manual_schedule())
        keep = ctx.enter_context(tc.tile_pool(name="keep", bufs=1))
        stage = ctx.enter_context(tc.tile_pool(name="stage", bufs=4))
        rope = ctx.enter_context(tc.tile_pool(name="rope", bufs=3))
        turned = ctx.enter_context(tc.tile_pool(name="turned", bufs=6))
        psum_scalar = ctx.enter_context(tc.psum_pool(name="psum_scalar", bufs=4))
        psum_vector = ctx.enter_context(tc.psum_pool(name="psum_vector", bufs=4))

        x_sb = keep.tile([P, BATCH, TOK_PER_PART, DIM], BF16)
        w_words = keep.tile([P, WEIGHTS, PASSES, 2 * HEADS * HEAD_DIM], U8, align_bytes=64)
        w_planes = keep.tile([P, WEIGHTS, PASSES, HEADS * HEAD_DIM], U8, align_bytes=64)
        bias_rows = keep.tile([P, P], BF16)
        zero = keep.tile([P, 1], F32)

        idle_in = keep.tile([P, TOKENS], BF16)
        nc.vector.memset(idle_in[:], 0.0)

        def keep_tensor_engine_busy(times):
            for i in range(times):
                idle_out = psum_vector.tile([P, TOKENS], F32, name="idle_out", tag="q")
                nc.tensor.matmul(
                    out=idle_out[:], lhsT=idle_in[:, 0:P], rhs=idle_in[:], start=True, stop=True
                )

        keep_tensor_engine_busy(IDLE_BEFORE_X)

        nc.vector.memset(w_planes[:].bitcast(I32), 0)
        nc.vector.memset(zero[:], 0.0)
        nc.gpsimd.memset(bias_rows[:], 0.0)

        def load_x(n):
            rows = x[n].rearrange("(p j) k -> p j k", j=TOK_PER_PART)
            for j in range(TOK_PER_PART):
                nc.sync.dma_start(out=x_sb[:, n, j, :], in_=rows[:, j, :])

        def load_weight(w):
            words, scales, bias = given[w]
            by_r = scales.bitcast(I32).rearrange("g (q r) n -> r q g n", r=4)
            for r in range(4):
                nc.sync.dma_start(out=w_planes[r:P:32, w, :, :].bitcast(I32), in_=by_r[r])
            nc.sync.dma_start(
                out=w_words[:, w, :, :].bitcast(I32),
                in_=words.bitcast(I32).rearrange("g p c -> p g c"),
            )
            nc.scalar.dma_start(
                out=bias_rows[HEADS * w : HEADS * (w + 1), :],
                in_=bias.rearrange("(h d) -> h d", d=HEAD_DIM),
            )

        load_x(0)
        load_weight(0)
        load_weight(1)
        load_x(1)

        nc.scalar.activation(out=zero[:], in_=zero[:], func=ACT.Sin)

        token_i = keep.tile([P, TOK_PER_PART], I32)
        nc.gpsimd.iota(token_i[:], pattern=[[1, TOK_PER_PART]], base=0, channel_multiplier=TOK_PER_PART)
        ident = keep.tile([P, P], F32)
        make_identity(nc, ident[:])
        bias_f32 = keep.tile([P, P], F32)
        nc.gpsimd.tensor_copy(out=bias_f32[:], in_=bias_rows[:])

        freq = keep.tile([P, FREQS], F32)
        nc.vector.memset(freq[:, 0:1], -1.0)
        s = 1
        while s < FREQS:
            factor = ROPE_BASE ** (-s / FREQS)
            nc.vector.tensor_scalar(
                out=freq[:, s : 2 * s], in0=freq[:, 0:s],
                scalar1=(-factor if s == 1 else factor), scalar2=None, op0=ALU.mult,
            )
            s *= 2

        table_shape = [P, TOK_PER_PART, FREQS]
        token_f = keep.tile([P, TOK_PER_PART], F32)
        nc.vector.tensor_copy(out=token_f[:], in_=token_i[:])
        turns = keep.tile(table_shape, F32)
        nc.vector.scalar_tensor_tensor(
            out=turns[:],
            in0=freq[:].unsqueeze(1).to_broadcast(table_shape),
            scalar=1.0 / TWO_PI,
            in1=token_f[:].unsqueeze(2).to_broadcast(table_shape),
            op0=ALU.mult,
            op1=ALU.mult,
        )
        shifted = keep.tile(table_shape, F32)
        nc.vector.tensor_scalar(
            out=shifted[:], in0=turns[:], scalar1=ROUND_TO_INT, scalar2=None, op0=ALU.add
        )
        flat = "p j m -> p (j m)"
        minus_frac = keep.tile(table_shape, F32)
        nc.vector.scalar_tensor_tensor(
            out=minus_frac[:].rearrange(flat), in0=shifted[:].rearrange(flat), scalar=ROUND_TO_INT,
            in1=turns[:].rearrange(flat), op0=ALU.subtract, op1=ALU.subtract,
        )
        for_cos = keep.tile(table_shape, F32)
        nc.vector.scalar_tensor_tensor(
            out=for_cos[:].rearrange(flat), in0=minus_frac[:].rearrange(flat), scalar=-1.0,
            in1=minus_frac[:].rearrange(flat), op0=ALU.mult, op1=ALU.min,
        )
        nc.vector.tensor_scalar(
            out=for_cos[:], in0=for_cos[:], scalar1=0.25, scalar2=None, op0=ALU.add
        )

        swap = keep.tile([P, P], F32)
        nc.vector.tensor_copy(
            out=swap[:].rearrange("p (c e) -> p c e", e=2),
            in_=ident[:].rearrange("p (c e) -> p c e", e=2)[:, :, ::-1],
        )

        x_codes = keep.tile([P, BATCH, PASSES, TOKENS], U32, align_bytes=64)
        x_planes = keep.tile([P, BATCH, PASSES, TOKENS], U8, align_bytes=64)

        def turn_and_quantise(n, j):
            words = x_sb[:, n, j, :].bitcast(F32)
            turned = psum_scalar.tile([P, PASSES, 2, P], F32, name="x_turned", tag="scalar")
            for g in range(PASSES):
                for u in range(2):
                    nc.tensor.transpose(
                        turned[:, g, u, :], words[:, 256 * g + u : 256 * (g + 1) : 2], ident[:]
                    )
            grouped = stage.tile([P, PASSES, 4 * P], BF16, name="grouped", align_bytes=64)
            nc.scalar.copy(
                out=grouped[:].bitcast(F32).rearrange("p g (t u) -> p g t u", u=2),
                in_=turned[:].rearrange("p g u t -> p g t u"),
            )
            cols = slice(P * j, P * (j + 1))
            for g in range(PASSES):
                nc.vector.quantize_mx(
                    out=x_codes[:, n, g, cols].bitcast(FP8X4),
                    scales=x_planes[:, n, g, cols],
                    in_=grouped[:, g, :],
                )

        for j in range(TOK_PER_PART):
            turn_and_quantise(0, j)
            keep_tensor_engine_busy(1)

        bias_turned = psum_scalar.tile([P, P], F32, name="bias_turned", tag="scalar")
        nc.tensor.transpose(bias_turned[:], bias_f32[:], ident[:])
        keep_tensor_engine_busy(IDLE_BEFORE_MX)
        bias_col = keep.tile([P, WEIGHTS * HEADS], F32)
        nc.scalar.copy(out=bias_col[:], in_=bias_turned[:, 0 : WEIGHTS * HEADS])

        tables = keep.tile([P, 2, TOK_PER_PART, 2, FREQS], F32)
        cos_tab = tables[:, 0]
        nc.scalar.activation(
            out=cos_tab,
            in_=for_cos[:].unsqueeze(2).to_broadcast([P, TOK_PER_PART, 2, FREQS]),
            func=ACT.Sin,
            scale=TWO_PI,
        )
        sin_tab = tables[:, 1]
        neighbour = minus_frac[:].rearrange("p j (i e) -> p j i e", e=2)[:, :, :, ::-1]
        for half in range(2):
            nc.scalar.activation(
                out=sin_tab[:, :, half, :].rearrange("p j (i e) -> p j i e", e=2),
                in_=neighbour,
                func=ACT.Sin,
                scale=-TWO_PI,
            )

        def project(n, w, first_head):
            biased = []
            for h in range(first_head, first_head + PAIR):
                acc = psum_scalar.tile([P, TOKENS], F32, name="acc", tag="scalar")
                for g in range(PASSES):
                    nc.tensor.matmul_mx(
                        out=acc[:],
                        lhsT=w_words[:, w, g, 2 * P * h : 2 * P * (h + 1)].bitcast(FP4X4),
                        lhsT_scale=w_planes[:, w, g, P * h : P * (h + 1)],
                        rhs=x_codes[:, n, g, :].bitcast(FP8X4),
                        rhs_scale=x_planes[:, n, g, :],
                        start=(g == 0),
                        stop=(g == PASSES - 1),
                    )
                q_t = stage.tile([P, TOKENS], F32, name="q_t")
                column = HEADS * w + h
                nc.scalar.activation(
                    out=q_t[:], in_=acc[:], func=ACT.Identity,
                    bias=bias_col[:, column : column + 1], scale=1.0,
                )
                biased.append(q_t)
            return biased

        def multiply(biased):
            q_tiles = []
            for q_t in biased:
                q = psum_vector.tile([P, TOK_PER_PART, HEAD_DIM], F32, name="q")
                for j in range(TOK_PER_PART):
                    nc.tensor.transpose(q[:, j, :], q_t[:, P * j : P * (j + 1)], ident[:])
                q_tiles.append(q)
            products = rope.tile([P, PAIR, 2, COUPLES, 2], F32, name="products")
            for a in range(PAIR):
                nc.vector.tensor_tensor(
                    out=products[:, a].rearrange("p k c e -> p k (c e)"),
                    in0=q_tiles[a][:]
                    .rearrange("p j d -> p (j d)")
                    .unsqueeze(1)
                    .to_broadcast([P, 2, TOK_PER_PART * HEAD_DIM]),
                    in1=tables[:].rearrange("p k j s m -> p k (j s m)"),
                    op=ALU.mult,
                )
            return products

        def finish(engine, heads_at_once, n, w, first_head, products):
            result = rope.tile([P, PAIR, COUPLES, 2], F32, name="result")
            for first in range(0, PAIR, heads_at_once):
                heads = slice(first, first + heads_at_once)
                engine.tensor_tensor(
                    out=result[:, heads],
                    in0=products[:, heads, 0],
                    in1=products[:, heads, 1, :, ::-1],
                    op=ALU.add,
                )
                for a in range(first, first + heads_at_once):
                    nc.sync.dma_start(
                        out=outs[w][n, first_head + a].rearrange(
                            "(p j) d -> p (j d)", j=TOK_PER_PART
                        ),
                        in_=result[:, a].rearrange("p c e -> p (c e)"),
                    )

        tables_turned = keep.tile([P, 2, TOKENS], F32)

        def turn_tables():
            for k in range(2):
                bank = psum_scalar.tile([P, TOK_PER_PART, P], F32, name="table_bank", tag="scalar")
                for j in range(TOK_PER_PART):
                    nc.tensor.transpose(
                        bank[:, j, :], tables[:, k, j].rearrange("p s m -> p (s m)"), ident[:]
                    )
                nc.scalar.copy(
                    out=tables_turned[:, k, :], in_=bank[:].rearrange("p j t -> p (j t)")
                )

        def turned_project(n, w, first_head):
            sums = []
            for h in range(first_head, first_head + PAIR):
                acc = psum_vector.tile([P, TOKENS], F32, name="acc_v", tag="q")
                for g in range(PASSES):
                    nc.tensor.matmul_mx(
                        out=acc[:],
                        lhsT=w_words[:, w, g, 2 * P * h : 2 * P * (h + 1)].bitcast(FP4X4),
                        lhsT_scale=w_planes[:, w, g, P * h : P * (h + 1)],
                        rhs=x_codes[:, n, g, :].bitcast(FP8X4),
                        rhs_scale=x_planes[:, n, g, :],
                        start=(g == 0),
                        stop=(g == PASSES - 1),
                    )
                sums.append(acc)
            return sums

        def turned_multiply(n, w, first_head, sums, size=PAIR):
            made = []
            for a in range(size):
                column = HEADS * w + first_head + a
                both = turned.tile([P, 2, TOKENS], F32, name="both")
                nc.vector.scalar_tensor_tensor(
                    out=both[:],
                    in0=sums[a][:].unsqueeze(1).to_broadcast([P, 2, TOKENS]),
                    scalar=bias_col[:, column : column + 1],
                    in1=tables_turned[:],
                    op0=ALU.add,
                    op1=ALU.mult,
                )
                made.append(both)
            return made

        def turned_finish(n, w, first_head, made, size=PAIR):
            for a in range(size):
                summed = psum_scalar.tile([P, TOK_PER_PART, HEAD_DIM], F32, name="summed", tag="scalar")
                for j in range(TOK_PER_PART):
                    cols = slice(P * j, P * (j + 1))
                    nc.tensor.matmul(
                        out=summed[:, j, :], lhsT=made[a][:, 0, cols], rhs=ident[:],
                        is_transpose=True, start=True, stop=False,
                    )
                    nc.tensor.matmul(
                        out=summed[:, j, :], lhsT=made[a][:, 1, cols], rhs=swap[:],
                        is_transpose=True, start=False, stop=True,
                    )
                turned_result = turned.tile([P, TOK_PER_PART * HEAD_DIM], F32, name="turned_result")
                nc.scalar.copy(out=turned_result[:], in_=summed[:].rearrange("p j d -> p (j d)"))
                nc.sync.dma_start(
                    out=outs[w][n, first_head + a].rearrange("(p j) d -> p (j d)", j=TOK_PER_PART),
                    in_=turned_result[:],
                )

        def turned_in_pieces(n, w, h, acc):
            column = HEADS * w + h
            rows = outs[w][n, h].rearrange("(p j) d -> p j d", j=TOK_PER_PART)
            for j in range(TOK_PER_PART):
                cols = slice(P * j, P * (j + 1))
                piece = turned.tile([P, 2, P], F32, name="piece")
                nc.vector.scalar_tensor_tensor(
                    out=piece[:],
                    in0=acc[:, cols].unsqueeze(1).to_broadcast([P, 2, P]),
                    scalar=bias_col[:, column : column + 1],
                    in1=tables_turned[:, :, cols],
                    op0=ALU.add,
                    op1=ALU.mult,
                )
                summed = psum_scalar.tile([P, HEAD_DIM], F32, name="summed_piece", tag="scalar")
                nc.tensor.matmul(
                    out=summed[:], lhsT=piece[:, 0, :], rhs=ident[:],
                    is_transpose=True, start=True, stop=False,
                )
                nc.tensor.matmul(
                    out=summed[:], lhsT=piece[:, 1, :], rhs=swap[:],
                    is_transpose=True, start=False, stop=True,
                )
                piece_result = turned.tile([P, HEAD_DIM], F32, name="piece_result")
                nc.scalar.copy(out=piece_result[:], in_=summed[:])
                nc.sync.dma_start(out=rows[:, j, :], in_=piece_result[:])

        groups = [
            (n, w, first_head)
            for n in range(BATCH)
            for w in range(WEIGHTS)
            for first_head in range(0, HEADS, PAIR)
        ]
        last = len(groups) - 1
        first_turned = len(groups) - TENSOR_ADDS

        def step_one(i):
            if i < first_turned:
                return project(*groups[i])
            return turned_project(*groups[i])

        def step_two(i, projected):
            if i < first_turned:
                finish(nc.gpsimd, PAIR, *groups[i], multiply(projected))
                return None
            return turned_multiply(*groups[i], projected)

        def step_three(i, made):
            if made is not None:
                turned_finish(*groups[i], made)

        step_two(0, step_one(0))
        waiting = step_one(1)
        made_before = None
        for i in range(2, len(groups)):
            projected = step_one(i)
            made = step_two(i - 1, waiting)
            step_three(i - 2, made_before)
            if i - 2 < TOK_PER_PART:
                turn_and_quantise(1, i - 2)
            if i == TOK_PER_PART + 2:
                turn_tables()
            waiting = projected
            made_before = made
        made = turned_multiply(*groups[last], waiting, 1)
        step_three(last - 1, made_before)
        turned_finish(*groups[last], made, 1)
        turned_in_pieces(groups[last][0], groups[last][1], groups[last][2] + 1, waiting[1])
